import numpy as np
import ml_dtypes


BF16 = ml_dtypes.bfloat16


def bf(x):
    return np.asarray(x, np.float32).astype(BF16)


def f64(x):
    return np.asarray(x).astype(np.float64)


E2M1 = np.array([0.0, 0.5, 1.0, 1.5, 2.0, 3.0, 4.0, 6.0, -0.0, -0.5, -1.0, -1.5, -2.0, -3.0, -4.0, -6.0])


def pack_weight(w, fmt):
    k, n = w.shape
    w = f64(bf(w)).reshape(k // 32, 32, n)
    amax = np.abs(w).max(1)
    if fmt == "e4m3":
        byte = np.frexp(amax)[1] - 1 + 127 - 7
    else:
        mant, ex = np.frexp(amax / 6.0)
        byte = np.where(mant > 0.5, ex, ex - 1) + 127
    byte = np.clip(np.where(amax > 0, byte, 1), 1, 254)
    scaled = (w * np.exp2(127.0 - byte)[:, None, :]).reshape(k, n).astype(np.float32)
    by_word = np.ascontiguousarray(scaled.reshape(k // 512, 128, 4, n).transpose(0, 1, 3, 2))
    if fmt == "e4m3":
        words = by_word.astype(ml_dtypes.float8_e4m3fn).view(np.uint8)
    else:
        c = by_word.astype(ml_dtypes.float4_e2m1fn).view(np.uint8) & 0xF
        words = c[..., 0::2] | (c[..., 1::2] << 4)
    return np.ascontiguousarray(words), np.ascontiguousarray(byte.astype(np.uint8).reshape(k // 512, 16, n))


def unpack_weight(words, scales, fmt):
    g, p, n, _ = words.shape
    if fmt == "e4m3":
        vals = np.ascontiguousarray(words).view(ml_dtypes.float8_e4m3fn).astype(np.float64)
    else:
        nib = np.empty((g, p, n, 4), np.uint8)
        nib[..., 0::2] = words & 0xF
        nib[..., 1::2] = words >> 4
        vals = E2M1[nib]
    vals = vals * np.repeat(np.exp2(scales.astype(np.float64) - 127.0), 8, axis=1)[..., None]
    return vals.transpose(0, 1, 3, 2).reshape(g * 512, n)

def pack4(w):
    words, scales = pack_weight(w, "e2m1")
    return words.reshape(words.shape[0], 128, -1), scales


def unpack4(words, scales):
    return unpack_weight(words.reshape(words.shape[0], 128, -1, 2), scales, "e2m1")


def kspread(k):
    return np.exp2(np.repeat(np.random.randint(-6, 7, k // 32), 32).astype(np.float64))


B, SA, SB, D, H, DH = 1, 128, 128, 2560, 8, 320
S = SA + SB
EPS = 1e-6


def make_rope(s, dh):
    pos = np.arange(s, dtype=np.float64)
    inv_freq = 1.0 / (10000.0 ** (np.arange(0, dh, 2, dtype=np.float64) / dh))
    theta = pos[:, None] * inv_freq[None, :]
    cos, sin = np.cos(theta), np.sin(theta)
    row0 = np.stack([cos, -sin], axis=-1)
    row1 = np.stack([sin, cos], axis=-1)
    return np.stack([row0, row1], axis=-2)[None, None]


def rms_norm(x, w):
    return x * (1.0 / np.sqrt(np.mean(x * x, axis=-1, keepdims=True) + EPS)) * w


def apply_rope(x, freqs):
    x_ = x.reshape(*x.shape[:-1], -1, 1, 2)
    out = freqs[..., 0] * x_[..., 0] + freqs[..., 1] * x_[..., 1]
    return out.reshape(x.shape)


def qkv(x, w_kn, b):
    y = (x @ w_kn) + b
    y = y.reshape(x.shape[0], x.shape[1], 3 * H, DH).transpose(0, 2, 1, 3)
    return y[:, :H], y[:, H:2 * H], y[:, 2 * H:]


def setup_inputs():
    sa, sb = kspread(D), kspread(D)
    hidden_states_a = np.random.standard_normal((B, SA, D)) * sa
    hidden_states_b = np.random.standard_normal((B, SB, D)) * sb
    image_rotary_emb = bf(make_rope(S, DH))
    a_w = np.random.standard_normal((3 * D, D)) / np.sqrt(D) / sa
    a_qkv_b = bf(np.random.standard_normal(3 * D) * 0.2)
    b_w = np.random.standard_normal((3 * D, D)) / np.sqrt(D) / sb
    b_qkv_b = bf(np.random.standard_normal(3 * D) * 0.2)
    a_words, a_scales = pack4(np.ascontiguousarray(a_w.T))
    b_words, b_scales = pack4(np.ascontiguousarray(b_w.T))
    hidden_states_a_words, hidden_states_a_scales = pack4(np.ascontiguousarray(hidden_states_a.reshape(B * SA, D).T))
    hidden_states_b_words, hidden_states_b_scales = pack4(np.ascontiguousarray(hidden_states_b.reshape(B * SB, D).T))
    return {
        "hidden_states_a_words": hidden_states_a_words,
        "hidden_states_a_scales": hidden_states_a_scales,
        "hidden_states_b_words": hidden_states_b_words,
        "hidden_states_b_scales": hidden_states_b_scales,
        "image_rotary_emb": image_rotary_emb,
        "a_qkv_w_words": a_words,
        "a_qkv_w_scales": a_scales,
        "a_qkv_b": a_qkv_b,
        "b_qkv_w_words": b_words,
        "b_qkv_w_scales": b_scales,
        "b_qkv_b": b_qkv_b,
        "norm_q_a_w": bf(1.5 + 0.15 * np.random.standard_normal(DH)),
        "norm_k_a_w": bf(1.5 + 0.15 * np.random.standard_normal(DH)),
        "norm_q_b_w": bf(1.5 + 0.15 * np.random.standard_normal(DH)),
        "norm_k_b_w": bf(1.5 + 0.15 * np.random.standard_normal(DH)),
    }


def reference(hidden_states_a_words, hidden_states_a_scales, hidden_states_b_words, hidden_states_b_scales,
              image_rotary_emb, a_qkv_w_words, a_qkv_w_scales, a_qkv_b,
              b_qkv_w_words, b_qkv_w_scales, b_qkv_b, norm_q_a_w, norm_k_a_w, norm_q_b_w, norm_k_b_w):
    x_a = unpack4(hidden_states_a_words, hidden_states_a_scales).T.reshape(B, SA, D)
    x_b = unpack4(hidden_states_b_words, hidden_states_b_scales).T.reshape(B, SB, D)
    q_a, k_a, v_a = qkv(x_a, unpack4(a_qkv_w_words, a_qkv_w_scales), f64(a_qkv_b))
    q_a = rms_norm(q_a, f64(norm_q_a_w))
    k_a = rms_norm(k_a, f64(norm_k_a_w))
    q_b, k_b, v_b = qkv(x_b, unpack4(b_qkv_w_words, b_qkv_w_scales), f64(b_qkv_b))
    q_b = rms_norm(q_b, f64(norm_q_b_w))
    k_b = rms_norm(k_b, f64(norm_k_b_w))
    q = np.concatenate([q_b, q_a], axis=2)
    k = np.concatenate([k_b, k_a], axis=2)
    v = np.concatenate([v_b, v_a], axis=2)
    f = f64(image_rotary_emb)
    return apply_rope(q, f), apply_rope(k, f), v

@@ -1,0 +1,268 @@
+from contextlib import ExitStack
+
+import concourse.mybir as mybir
+from concourse.masks import make_identity
+
+F32 = mybir.dt.float32
+BF16 = mybir.dt.bfloat16
+I32 = mybir.dt.int32
+U8 = mybir.dt.uint8
+FP4X4 = mybir.dt.float4_e2m1fn_x4
+ACT = mybir.ActivationFunctionType
+ALU = mybir.AluOpType
+
+P = 128
+TOKENS = 128
+D = 2560
+HEADS = 8
+DH = 320
+PAIRS = DH // 2
+EPS = 1e-6
+PASSES = D // 512
+BANK = 512
+ROW = 512
+UNIT = 1024
+
+FLOPS = 2 * 2 * TOKENS * D * 3 * D
+
+Q, K, V = 0, 1, 2
+A, B = 0, 1
+
+CHUNKS = (
+    [(A, Q, 0, 2), (A, Q, 2, 2), (A, Q, 4, 4), (A, K, 0, 4), (A, K, 4, 4)]
+    + [(B, Q, 0, 4), (B, Q, 4, 4), (B, K, 0, 4), (B, K, 4, 4)]
+    + [(A, V, 0, 4), (A, V, 4, 4), (B, V, 0, 4), (B, V, 4, 2), (B, V, 6, 2)]
+)
+RING = 6
+AHEAD = 6
+
+
+def tile_fluxjointattention_pa_kernel(
+    tc, xa_words, xa_scales, xb_words, xb_scales, rope, wa_words, wa_scales, a_bias,
+    wb_words, wb_scales, b_bias, gain_qa, gain_ka, gain_qb, gain_kb, out_q, out_k, out_v,
+):
+    nc = tc.nc
+    x_words, x_scales = (xa_words, xb_words), (xa_scales, xb_scales)
+    w_words, w_scales = (wa_words, wb_words), (wa_scales, wb_scales)
+    outs = (out_q, out_k, out_v)
+    first_pos = (TOKENS, 0)
+    gains = ((gain_qa, gain_ka), (gain_qb, gain_kb))
+
+    with ExitStack() as ctx:
+        keep = ctx.enter_context(tc.tile_pool(name="keep", bufs=1))
+        codes_pool = ctx.enter_context(tc.tile_pool(name="codes", bufs=RING))
+        small_pool = ctx.enter_context(tc.tile_pool(name="small_codes", bufs=2))
+        work = ctx.enter_context(tc.tile_pool(name="work", bufs=2))
+        result = ctx.enter_context(tc.tile_pool(name="result", bufs=4))
+        stats = ctx.enter_context(tc.tile_pool(name="stats", bufs=4))
+        acc_pool = ctx.enter_context(tc.psum_pool(name="acc", bufs=6))
+        row_pool = ctx.enter_context(tc.psum_pool(name="rowbank", bufs=2))
+        ctx.enter_context(tc.manual_schedule())
+
+        xw = [keep.tile([P, PASSES, 2 * TOKENS], U8, name="xw%d" % s, align_bytes=256) for s in (A, B)]
+        xs = [keep.tile([P, PASSES, TOKENS], U8, name="xs%d" % s, align_bytes=256) for s in (A, B)]
+        big = [keep.tile([P, PASSES, 4 * DH], U8, name="plane%d" % i, align_bytes=256) for i in range(RING)]
+        little = [keep.tile([P, PASSES, 2 * DH], U8, name="small_plane%d" % i, align_bytes=256) for i in range(2)]
+        rows = [keep.tile([P, ROW], BF16, name="rows%d" % i) for i in range(3)]
+        bias = keep.tile([P, 2 * 3 * D], BF16, name="bias")
+        ident = keep.tile([P, P], BF16, name="ident")
+        f_raw = [keep.tile([P, 4 * PAIRS], BF16, name="f_raw%d" % s) for s in (A, B)]
+        tables = [[keep.tile([P, 2, PAIRS, 2], F32, name="table%d%d" % (s, t)) for t in (Q, K)] for s in (A, B)]
+
+        def clear(engine, t):
+            engine.memset(t[:].rearrange("p g n -> p (g n)").bitcast(I32), 0)
+
+        def load_x(s):
+            nc.sync.dma_start(
+                out=xw[s][:].bitcast(I32), in_=x_words[s].rearrange("g p n -> p g n").bitcast(I32)
+            )
+
+        def load_x_scales(s):
+            for q in range(4):
+                nc.sync.dma_start(
+                    out=xs[s][32 * q : 32 * q + 4, :, :].bitcast(I32),
+                    in_=x_scales[s][:, 4 * q : 4 * q + 4, :].rearrange("g q n -> q g n").bitcast(I32),
+                )
+
+        loaded = {}
+        counts = {2: 0, 4: 0}
+
+        def load_codes(c):
+            s, kind, h0, nh = CHUNKS[c]
+            n = nh * DH
+            c0 = (kind * HEADS + h0) * DH
+            if nh == 4:
+                codes = codes_pool.tile([P, PASSES, 2 * n], U8, name="codes", align_bytes=256)
+                plane = big[counts[4] % RING]
+            else:
+                codes = small_pool.tile([P, PASSES, 2 * n], U8, name="scodes", align_bytes=256)
+                plane = little[counts[2] % 2]
+            counts[nh] += 1
+            nc.sync.dma_start(
+                out=codes[:].bitcast(I32),
+                in_=w_words[s][:, :, 2 * c0 : 2 * (c0 + n)].rearrange("g p n -> p g n").bitcast(I32),
+            )
+            loaded[c] = (codes, plane)
+
+        def load_scales(c):
+            s, kind, h0, nh = CHUNKS[c]
+            n = nh * DH
+            c0 = (kind * HEADS + h0) * DH
+            plane = loaded[c][1]
+            if c < 2:
+                for q in range(4):
+                    nc.sync.dma_start(
+                        out=plane[32 * q : 32 * q + 4, :, :].bitcast(I32),
+                        in_=w_scales[s][:, 4 * q : 4 * q + 4, c0 : c0 + n].rearrange("g q n -> q g n").bitcast(I32),
+                    )
+                return
+            for r in range(4):
+                nc.sync.dma_start(
+                    out=plane[r : P : 32, :, :].bitcast(I32),
+                    in_=w_scales[s][:, r : 16 : 4, c0 : c0 + n].rearrange("g q n -> q g n").bitcast(I32),
+                )
+
+        row_order = [(s, c) for part in (range(0, 10), range(10, 15)) for s in (A, B) for c in part]
+
+        def spread_bias(u):
+            bank = row_pool.tile([P, UNIT], BF16, name="row")
+            for i in range(2):
+                s, c = row_order[2 * u + i]
+                nc.tensor.matmul(
+                    bank[:, i * ROW : (i + 1) * ROW],
+                    lhsT=ident[:, c : c + 1].to_broadcast([P, P]), rhs=rows[s][:], start=True, stop=True,
+                )
+            nc.scalar.copy(out=bias[:, u * UNIT : (u + 1) * UNIT], in_=bank[:])
+
+        def make_table(s, t):
+            c = 2 * s + t
+            bank = row_pool.tile([P, ROW], F32, name="row")
+            nc.tensor.matmul(
+                bank[:, :DH], lhsT=ident[:, c : c + 1].to_broadcast([P, P]), rhs=rows[2][:, :DH], start=True, stop=True
+            )
+            nc.vector.tensor_tensor(
+                out=tables[s][t][:],
+                in0=f_raw[s][:].rearrange("p (j i t) -> p t j i", i=2, t=2),
+                in1=bank[:, :DH].rearrange("p (j t) -> p t j", t=2).unsqueeze(3).to_broadcast([P, 2, PAIRS, 2]),
+                op=ALU.mult,
+            )
+
+        load_x(A)
+        load_codes(0)
+        clear(nc.vector, xs[A])
+        for t in rows:
+            nc.vector.memset(t[:], 0.0)
+        clear(nc.vector, little[0])
+        load_x_scales(A)
+        load_scales(0)
+        rope_rows = rope.rearrange("o u s j i t -> (o u s) (j i t)")
+        nc.gpsimd.dma_start(out=rows[A][0:15, :], in_=a_bias.rearrange("(c n) -> c n", n=ROW))
+        make_identity(nc, ident[:])
+        for s in (A, B):
+            for t in (Q, K):
+                nc.gpsimd.dma_start(out=rows[2][2 * s + t : 2 * s + t + 1, :DH], in_=gains[s][t].unsqueeze(0))
+        nc.gpsimd.dma_start(out=f_raw[A][:], in_=rope_rows[TOKENS : 2 * TOKENS, :])
+        clear(nc.vector, little[1])
+        clear(nc.vector, big[0])
+        clear(nc.gpsimd, big[1])
+        nc.gpsimd.dma_start(out=rows[B][0:15, :], in_=b_bias.rearrange("(c n) -> c n", n=ROW))
+        nc.gpsimd.dma_start(out=f_raw[B][:], in_=rope_rows[0:TOKENS, :])
+        for i in range(2, RING):
+            clear(nc.gpsimd, big[i])
+        clear(nc.vector, xs[B])
+        load_codes(1)
+        load_scales(1)
+        load_codes(2)
+        load_scales(2)
+        spread_bias(0)
+        load_x(B)
+        load_x_scales(B)
+        for c in range(3, AHEAD):
+            load_codes(c)
+            load_scales(c)
+
+        pos = 0
+        unit = 1
+        ends = [sum(m[3] for m in CHUNKS[: c + 1]) * DH for c in range(len(CHUNKS))] + [2 * 3 * D]
+        for c in range(len(CHUNKS)):
+            s, kind, h0, nh = CHUNKS[c]
+            n = nh * DH
+            codes, plane = loaded[c]
+            widths = [BANK, 128] if nh == 2 else [BANK, BANK, 256]
+            banks = []
+            c0 = 0
+            for w in widths:
+                acc = acc_pool.tile([P, BANK], F32, name="acc")
+                for g in range(PASSES):
+                    nc.tensor.matmul_mx(
+                        out=acc[:, :w],
+                        lhsT=xw[s][:, g, :].bitcast(FP4X4), lhsT_scale=xs[s][:, g, :],
+                        rhs=codes[:, g, 2 * c0 : 2 * (c0 + w)].bitcast(FP4X4), rhs_scale=plane[:, g, c0 : c0 + w],
+                        start=(g == 0), stop=(g == PASSES - 1),
+                    )
+                banks.append((acc, c0, w))
+                c0 += w
+            if c + AHEAD < len(CHUNKS):
+                load_codes(c + AHEAD)
+                load_scales(c + AHEAD)
+
+            if c == 0:
+                for t in (Q, K):
+                    make_table(A, t)
+
+            res = result.tile([P, 4 * DH], F32, name="res")
+            u = res if kind == V else work.tile([P, 4 * DH], F32, name="u")
+            for acc, c0, w in banks:
+                nc.vector.tensor_tensor(
+                    out=u[:, c0 : c0 + w], in0=acc[:, :w], in1=bias[:, pos + c0 : pos + c0 + w], op=ALU.add
+                )
+            pos += n
+            if kind != V:
+                ss = stats.tile([P, 4], F32, name="ss")
+                rs = stats.tile([P, 4], F32, name="rs")
+                for h in range(nh):
+                    junk = work.tile([P, DH], BF16, name="junk")
+                    nc.scalar.activation(
+                        out=junk[:], in_=u[:, h * DH : (h + 1) * DH], func=ACT.Square, accum_out=ss[:, h : h + 1]
+                    )
+                nc.scalar.activation(
+                    out=rs[:, :nh], in_=ss[:, :nh], func=ACT.Abs_reciprocal_sqrt, scale=1.0 / DH, bias=EPS
+                )
+                odd = work.tile([P, 4 * DH], F32, name="odd")
+                table = tables[s][kind]
+                halves = [(i, i + 2) for i in range(0, nh, 2)]
+
+                def view(t, lo, hi):
+                    return t[:, lo * DH : hi * DH].rearrange("p (h j i) -> p h j i", j=PAIRS, i=2)
+
+                for lo, hi in halves:
+                    shape = [P, hi - lo, PAIRS, 2]
+                    for t, dst in ((0, res), (1, odd)):
+                        nc.vector.tensor_tensor(
+                            out=view(dst, lo, hi),
+                            in0=view(u, lo, hi)[:, :, :, t : t + 1].to_broadcast(shape),
+                            in1=table[:, t, :, :].unsqueeze(1).to_broadcast(shape),
+                            op=ALU.mult,
+                        )
+                for lo, hi in halves:
+                    nc.vector.tensor_tensor(
+                        out=res[:, lo * DH : hi * DH], in0=res[:, lo * DH : hi * DH],
+                        in1=odd[:, lo * DH : hi * DH], op=ALU.add,
+                    )
+            if c == 3:
+                for t in (Q, K):
+                    make_table(B, t)
+            while unit * UNIT < ends[c + 1]:
+                spread_bias(unit)
+                unit += 1
+            if kind != V:
+                for h in range(nh):
+                    nc.scalar.activation(
+                        out=res[:, h * DH : (h + 1) * DH], in_=res[:, h * DH : (h + 1) * DH],
+                        func=ACT.Copy, scale=rs[:, h : h + 1],
+                    )
+            p0 = first_pos[s]
+            nc.gpsimd.dma_start(
+                out=outs[kind][0, h0 : h0 + nh, p0 : p0 + TOKENS, :].rearrange("h p d -> p h d"),
+                in_=res[:, :n].rearrange("p (h d) -> p h d", d=DH),
+            )

@@ -17,24 +17,20 @@ D = 2560
 HEADS = 8
 DH = 320
 PAIRS = DH // 2
+HALF = HEADS // 2
 EPS = 1e-6
 PASSES = D // 512
 BANK = 512
-ROW = 512
-UNIT = 1024
+BANKS = D // BANK
+GROUP = 2 * BANK
 
 FLOPS = 2 * 2 * TOKENS * D * 3 * D
 
 Q, K, V = 0, 1, 2
 A, B = 0, 1
-
-CHUNKS = (
-    [(A, Q, 0, 2), (A, Q, 2, 2), (A, Q, 4, 4), (A, K, 0, 4), (A, K, 4, 4)]
-    + [(B, Q, 0, 4), (B, Q, 4, 4), (B, K, 0, 4), (B, K, 4, 4)]
-    + [(A, V, 0, 4), (A, V, 4, 4), (B, V, 0, 4), (B, V, 4, 2), (B, V, 6, 2)]
-)
-RING = 6
-AHEAD = 6
+UNITS = [(A, Q), (A, K), (B, Q), (B, K), (A, V), (B, V)]
+SLOTS = 3
+PLANES = 4
 
 
 def tile_fluxjointattention_pa_kernel(
@@ -44,101 +40,82 @@ def tile_fluxjointattention_pa_kernel(
     nc = tc.nc
     x_words, x_scales = (xa_words, xb_words), (xa_scales, xb_scales)
     w_words, w_scales = (wa_words, wb_words), (wa_scales, wb_scales)
+    biases = (a_bias, b_bias)
     outs = (out_q, out_k, out_v)
     first_pos = (TOKENS, 0)
     gains = ((gain_qa, gain_ka), (gain_qb, gain_kb))
 
     with ExitStack() as ctx:
         keep = ctx.enter_context(tc.tile_pool(name="keep", bufs=1))
-        codes_pool = ctx.enter_context(tc.tile_pool(name="codes", bufs=RING))
-        small_pool = ctx.enter_context(tc.tile_pool(name="small_codes", bufs=2))
         work = ctx.enter_context(tc.tile_pool(name="work", bufs=2))
-        result = ctx.enter_context(tc.tile_pool(name="result", bufs=4))
+        result = ctx.enter_context(tc.tile_pool(name="result", bufs=3))
         stats = ctx.enter_context(tc.tile_pool(name="stats", bufs=4))
         acc_pool = ctx.enter_context(tc.psum_pool(name="acc", bufs=6))
         row_pool = ctx.enter_context(tc.psum_pool(name="rowbank", bufs=2))
         ctx.enter_context(tc.manual_schedule())
 
-        xw = [keep.tile([P, PASSES, 2 * TOKENS], U8, name="xw%d" % s, align_bytes=256) for s in (A, B)]
-        xs = [keep.tile([P, PASSES, TOKENS], U8, name="xs%d" % s, align_bytes=256) for s in (A, B)]
-        big = [keep.tile([P, PASSES, 4 * DH], U8, name="plane%d" % i, align_bytes=256) for i in range(RING)]
-        little = [keep.tile([P, PASSES, 2 * DH], U8, name="small_plane%d" % i, align_bytes=256) for i in range(2)]
-        rows = [keep.tile([P, ROW], BF16, name="rows%d" % i) for i in range(3)]
+        xw = [keep.tile([P, PASSES * 2 * TOKENS], U8, name="xw%d" % s, align_bytes=256) for s in (A, B)]
+        xs = [keep.tile([P, PASSES * TOKENS], U8, name="xs%d" % s, align_bytes=256) for s in (A, B)]
+        codes = [keep.tile([P, PASSES * 2 * D], U8, name="codes%d" % i, align_bytes=256) for i in range(SLOTS)]
+        planes = [keep.tile([P, PASSES * D], U8, name="plane%d" % i, align_bytes=256) for i in range(PLANES)]
+        rows = [keep.tile([P, BANK], BF16, name="rows%d" % s) for s in (A, B)]
+        gain_rows = [keep.tile([P, DH], BF16, name="gain_rows%d" % s) for s in (A, B)]
         bias = keep.tile([P, 2 * 3 * D], BF16, name="bias")
         ident = keep.tile([P, P], BF16, name="ident")
         f_raw = [keep.tile([P, 4 * PAIRS], BF16, name="f_raw%d" % s) for s in (A, B)]
         tables = [[keep.tile([P, 2, PAIRS, 2], F32, name="table%d%d" % (s, t)) for t in (Q, K)] for s in (A, B)]
 
         def clear(engine, t):
-            engine.memset(t[:].rearrange("p g n -> p (g n)").bitcast(I32), 0)
+            engine.memset(t[:].bitcast(I32), 0)
 
-        def load_x(s):
-            nc.sync.dma_start(
-                out=xw[s][:].bitcast(I32), in_=x_words[s].rearrange("g p n -> p g n").bitcast(I32)
-            )
+        def by_pass(ap):
+            return ap.rearrange("p (g n) -> p g n", g=PASSES).bitcast(I32)
 
-        def load_x_scales(s):
+        def load_tokens(s):
+            nc.sync.dma_start(out=by_pass(xw[s][:]), in_=x_words[s].rearrange("g p n -> p g n").bitcast(I32))
+
+        def load_token_scales(s):
             for q in range(4):
                 nc.sync.dma_start(
-                    out=xs[s][32 * q : 32 * q + 4, :, :].bitcast(I32),
+                    out=by_pass(xs[s][32 * q : 32 * q + 4, :]),
                     in_=x_scales[s][:, 4 * q : 4 * q + 4, :].rearrange("g q n -> q g n").bitcast(I32),
                 )
 
-        loaded = {}
-        counts = {2: 0, 4: 0}
-
-        def load_codes(c):
-            s, kind, h0, nh = CHUNKS[c]
-            n = nh * DH
-            c0 = (kind * HEADS + h0) * DH
-            if nh == 4:
-                codes = codes_pool.tile([P, PASSES, 2 * n], U8, name="codes", align_bytes=256)
-                plane = big[counts[4] % RING]
-            else:
-                codes = small_pool.tile([P, PASSES, 2 * n], U8, name="scodes", align_bytes=256)
-                plane = little[counts[2] % 2]
-            counts[nh] += 1
+        def load_codes(u, g):
+            s, kind = UNITS[u]
             nc.sync.dma_start(
-                out=codes[:].bitcast(I32),
-                in_=w_words[s][:, :, 2 * c0 : 2 * (c0 + n)].rearrange("g p n -> p g n").bitcast(I32),
+                out=codes[u % SLOTS][:, 2 * D * g : 2 * D * (g + 1)].bitcast(I32),
+                in_=w_words[s][g, :, 2 * D * kind : 2 * D * (kind + 1)].bitcast(I32),
             )
-            loaded[c] = (codes, plane)
 
-        def load_scales(c):
-            s, kind, h0, nh = CHUNKS[c]
-            n = nh * DH
-            c0 = (kind * HEADS + h0) * DH
-            plane = loaded[c][1]
-            if c < 2:
-                for q in range(4):
-                    nc.sync.dma_start(
-                        out=plane[32 * q : 32 * q + 4, :, :].bitcast(I32),
-                        in_=w_scales[s][:, 4 * q : 4 * q + 4, c0 : c0 + n].rearrange("g q n -> q g n").bitcast(I32),
-                    )
-                return
-            for r in range(4):
+        def load_scales(u, rs=range(4)):
+            s, kind = UNITS[u]
+            for r in rs:
                 nc.sync.dma_start(
-                    out=plane[r : P : 32, :, :].bitcast(I32),
-                    in_=w_scales[s][:, r : 16 : 4, c0 : c0 + n].rearrange("g q n -> q g n").bitcast(I32),
+                    out=by_pass(planes[u % PLANES][r : P : 32, :]),
+                    in_=w_scales[s][:, r : 16 : 4, D * kind : D * (kind + 1)].rearrange("g q n -> q g n").bitcast(I32),
                 )
 
-        row_order = [(s, c) for part in (range(0, 10), range(10, 15)) for s in (A, B) for c in part]
+        def load_unit(u):
+            for g in range(PASSES):
+                load_codes(u, g)
 
-        def spread_bias(u):
-            bank = row_pool.tile([P, UNIT], BF16, name="row")
+        row_order = [(s, kind * BANKS + i) for s, kind in UNITS for i in range(BANKS)]
+
+        def spread(group):
+            bank = row_pool.tile([P, GROUP], BF16, name="row")
             for i in range(2):
-                s, c = row_order[2 * u + i]
+                s, c = row_order[2 * group + i]
                 nc.tensor.matmul(
-                    bank[:, i * ROW : (i + 1) * ROW],
+                    bank[:, i * BANK : (i + 1) * BANK],
                     lhsT=ident[:, c : c + 1].to_broadcast([P, P]), rhs=rows[s][:], start=True, stop=True,
                 )
-            nc.scalar.copy(out=bias[:, u * UNIT : (u + 1) * UNIT], in_=bank[:])
+            nc.scalar.copy(out=bias[:, group * GROUP : (group + 1) * GROUP], in_=bank[:])
 
         def make_table(s, t):
-            c = 2 * s + t
-            bank = row_pool.tile([P, ROW], F32, name="row")
+            bank = row_pool.tile([P, BANK], F32, name="row")
             nc.tensor.matmul(
-                bank[:, :DH], lhsT=ident[:, c : c + 1].to_broadcast([P, P]), rhs=rows[2][:, :DH], start=True, stop=True
+                bank[:, :DH], lhsT=ident[:, t : t + 1].to_broadcast([P, P]), rhs=gain_rows[s][:], start=True, stop=True
             )
             nc.vector.tensor_tensor(
                 out=tables[s][t][:],
@@ -147,122 +124,184 @@ def tile_fluxjointattention_pa_kernel(
                 op=ALU.mult,
             )
 
-        load_x(A)
-        load_codes(0)
-        clear(nc.vector, xs[A])
-        for t in rows:
-            nc.vector.memset(t[:], 0.0)
-        clear(nc.vector, little[0])
-        load_x_scales(A)
-        load_scales(0)
-        rope_rows = rope.rearrange("o u s j i t -> (o u s) (j i t)")
-        nc.gpsimd.dma_start(out=rows[A][0:15, :], in_=a_bias.rearrange("(c n) -> c n", n=ROW))
-        make_identity(nc, ident[:])
-        for s in (A, B):
-            for t in (Q, K):
-                nc.gpsimd.dma_start(out=rows[2][2 * s + t : 2 * s + t + 1, :DH], in_=gains[s][t].unsqueeze(0))
-        nc.gpsimd.dma_start(out=f_raw[A][:], in_=rope_rows[TOKENS : 2 * TOKENS, :])
-        clear(nc.vector, little[1])
-        clear(nc.vector, big[0])
-        clear(nc.gpsimd, big[1])
-        nc.gpsimd.dma_start(out=rows[B][0:15, :], in_=b_bias.rearrange("(c n) -> c n", n=ROW))
-        nc.gpsimd.dma_start(out=f_raw[B][:], in_=rope_rows[0:TOKENS, :])
-        for i in range(2, RING):
-            clear(nc.gpsimd, big[i])
-        clear(nc.vector, xs[B])
-        load_codes(1)
-        load_scales(1)
-        load_codes(2)
-        load_scales(2)
-        spread_bias(0)
-        load_x(B)
-        load_x_scales(B)
-        for c in range(3, AHEAD):
-            load_codes(c)
-            load_scales(c)
-
-        pos = 0
-        unit = 1
-        ends = [sum(m[3] for m in CHUNKS[: c + 1]) * DH for c in range(len(CHUNKS))] + [2 * 3 * D]
-        for c in range(len(CHUNKS)):
-            s, kind, h0, nh = CHUNKS[c]
-            n = nh * DH
-            codes, plane = loaded[c]
-            widths = [BANK, 128] if nh == 2 else [BANK, BANK, 256]
-            banks = []
-            c0 = 0
-            for w in widths:
-                acc = acc_pool.tile([P, BANK], F32, name="acc")
-                for g in range(PASSES):
-                    nc.tensor.matmul_mx(
-                        out=acc[:, :w],
-                        lhsT=xw[s][:, g, :].bitcast(FP4X4), lhsT_scale=xs[s][:, g, :],
-                        rhs=codes[:, g, 2 * c0 : 2 * (c0 + w)].bitcast(FP4X4), rhs_scale=plane[:, g, c0 : c0 + w],
-                        start=(g == 0), stop=(g == PASSES - 1),
-                    )
-                banks.append((acc, c0, w))
-                c0 += w
-            if c + AHEAD < len(CHUNKS):
-                load_codes(c + AHEAD)
-                load_scales(c + AHEAD)
-
-            if c == 0:
-                for t in (Q, K):
-                    make_table(A, t)
-
-            res = result.tile([P, 4 * DH], F32, name="res")
-            u = res if kind == V else work.tile([P, 4 * DH], F32, name="u")
-            for acc, c0, w in banks:
-                nc.vector.tensor_tensor(
-                    out=u[:, c0 : c0 + w], in0=acc[:, :w], in1=bias[:, pos + c0 : pos + c0 + w], op=ALU.add
+        def multiply(u, banks, g):
+            s, kind = UNITS[u]
+            for b in range(BANKS):
+                at = g * D + b * BANK
+                nc.tensor.matmul_mx(
+                    out=banks[b][:],
+                    lhsT=xw[s][:, 2 * TOKENS * g : 2 * TOKENS * (g + 1)].bitcast(FP4X4),
+                    lhsT_scale=xs[s][:, TOKENS * g : TOKENS * (g + 1)],
+                    rhs=codes[u % SLOTS][:, 2 * at : 2 * (at + BANK)].bitcast(FP4X4),
+                    rhs_scale=planes[u % PLANES][:, at : at + BANK],
+                    start=(g == 0), stop=(g == PASSES - 1),
                 )
-            pos += n
-            if kind != V:
-                ss = stats.tile([P, 4], F32, name="ss")
-                rs = stats.tile([P, 4], F32, name="rs")
-                for h in range(nh):
+
+        def new_banks():
+            banks = []
+            for b in range(BANKS):
+                acc = acc_pool.tile([P, BANK], F32, name="acc")
+                banks.append(acc)
+            return banks
+
+        def store(u, h0, h1, tile, engine):
+            s, kind = UNITS[u]
+            p0 = first_pos[s]
+            engine.dma_start(
+                out=outs[kind][0, h0:h1, p0 : p0 + TOKENS, :].rearrange("h p d -> p h d"),
+                in_=tile.rearrange("p (h d) -> p h d", d=DH),
+            )
+
+        def add_bias(u, banks, y, b):
+            nc.vector.tensor_tensor(
+                out=y[:, b * BANK : (b + 1) * BANK], in0=banks[b][:],
+                in1=bias[:, u * D + b * BANK : u * D + (b + 1) * BANK], op=ALU.add,
+            )
+
+        def head_view(ap):
+            return ap.rearrange("p (h j i) -> p h j i", j=PAIRS, i=2)
+
+        def epilogue_v(u, banks):
+            y = work.tile([P, D], F32, name="y")
+            engine = nc.sync if u == len(UNITS) - 1 else nc.gpsimd
+            stores = {1: (0, 3), 3: (3, 6), 4: (6, 8)}
+
+            def part(b):
+                add_bias(u, banks, y, b)
+                if b in stores:
+                    h0, h1 = stores[b]
+                    store(u, h0, h1, y[:, h0 * DH : h1 * DH], engine)
+
+            return [lambda b=b: part(b) for b in range(BANKS)]
+
+        def epilogue_qk(u, banks):
+            s, kind = UNITS[u]
+            y = work.tile([P, D], F32, name="y")
+            ss = stats.tile([P, HEADS], F32, name="ss")
+            rs = stats.tile([P, HEADS], F32, name="rs")
+            table = tables[s][kind]
+            shape = [P, HALF, PAIRS, 2]
+            width = HALF * DH
+            halves = []
+
+            def squares(half):
+                for h in range(half * HALF, (half + 1) * HALF):
                     junk = work.tile([P, DH], BF16, name="junk")
                     nc.scalar.activation(
-                        out=junk[:], in_=u[:, h * DH : (h + 1) * DH], func=ACT.Square, accum_out=ss[:, h : h + 1]
+                        out=junk[:], in_=y[:, h * DH : (h + 1) * DH], func=ACT.Square, accum_out=ss[:, h : h + 1]
                     )
+                hs = slice(half * HALF, (half + 1) * HALF)
                 nc.scalar.activation(
-                    out=rs[:, :nh], in_=ss[:, :nh], func=ACT.Abs_reciprocal_sqrt, scale=1.0 / DH, bias=EPS
+                    out=rs[:, hs], in_=ss[:, hs], func=ACT.Abs_reciprocal_sqrt, scale=1.0 / DH, bias=EPS
                 )
-                odd = work.tile([P, 4 * DH], F32, name="odd")
-                table = tables[s][kind]
-                halves = [(i, i + 2) for i in range(0, nh, 2)]
 
-                def view(t, lo, hi):
-                    return t[:, lo * DH : hi * DH].rearrange("p (h j i) -> p h j i", j=PAIRS, i=2)
+            def product(half, t, dst):
+                nc.vector.tensor_tensor(
+                    out=head_view(dst[:]),
+                    in0=head_view(y[:, half * width : (half + 1) * width])[:, :, :, t : t + 1].to_broadcast(shape),
+                    in1=table[:, t, :, :].unsqueeze(1).to_broadcast(shape),
+                    op=ALU.mult,
+                )
 
-                for lo, hi in halves:
-                    shape = [P, hi - lo, PAIRS, 2]
-                    for t, dst in ((0, res), (1, odd)):
-                        nc.vector.tensor_tensor(
-                            out=view(dst, lo, hi),
-                            in0=view(u, lo, hi)[:, :, :, t : t + 1].to_broadcast(shape),
-                            in1=table[:, t, :, :].unsqueeze(1).to_broadcast(shape),
-                            op=ALU.mult,
-                        )
-                for lo, hi in halves:
-                    nc.vector.tensor_tensor(
-                        out=res[:, lo * DH : hi * DH], in0=res[:, lo * DH : hi * DH],
-                        in1=odd[:, lo * DH : hi * DH], op=ALU.add,
-                    )
-            if c == 3:
-                for t in (Q, K):
-                    make_table(B, t)
-            while unit * UNIT < ends[c + 1]:
-                spread_bias(unit)
-                unit += 1
-            if kind != V:
-                for h in range(nh):
+            def finish(half):
+                res, odd = halves[half]
+                nc.vector.tensor_tensor(out=res[:], in0=res[:], in1=odd[:], op=ALU.add)
+
+            def scale_and_store(half):
+                res, odd = halves[half]
+                for i in range(HALF):
+                    h = half * HALF + i
                     nc.scalar.activation(
-                        out=res[:, h * DH : (h + 1) * DH], in_=res[:, h * DH : (h + 1) * DH],
+                        out=res[:, i * DH : (i + 1) * DH], in_=res[:, i * DH : (i + 1) * DH],
                         func=ACT.Copy, scale=rs[:, h : h + 1],
                     )
-            p0 = first_pos[s]
-            nc.gpsimd.dma_start(
-                out=outs[kind][0, h0 : h0 + nh, p0 : p0 + TOKENS, :].rearrange("h p d -> p h d"),
-                in_=res[:, :n].rearrange("p (h d) -> p h d", d=DH),
-            )
+                store(u, half * HALF, (half + 1) * HALF, res[:], nc.gpsimd)
+
+            def start_half(half):
+                res = result.tile([P, width], F32, name="res")
+                odd = work.tile([P, width], F32, name="odd")
+                halves.append((res, odd))
+
+            def part0():
+                for b in range(BANKS):
+                    add_bias(u, banks, y, b)
+                squares(0)
+
+            def part1():
+                start_half(0)
+                product(0, 0, halves[0][0])
+                product(0, 1, halves[0][1])
+                squares(1)
+
+            def part2():
+                start_half(1)
+                product(1, 0, halves[1][0])
+                finish(0)
+                scale_and_store(0)
+
+            def part3():
+                product(1, 1, halves[1][1])
+                finish(1)
+
+            def part4():
+                scale_and_store(1)
+
+            return [part0, part1, part2, part3, part4]
+
+        load_tokens(A)
+        load_codes(0, 0)
+        clear(nc.vector, xs[A])
+        for t in rows + gain_rows:
+            nc.vector.memset(t[:], 0.0)
+        clear(nc.vector, planes[0])
+        load_token_scales(A)
+        load_codes(0, 1)
+        load_scales(0)
+        rope_rows = rope.rearrange("o u s j i t -> (o u s) (j i t)")
+        for s in (A, B):
+            nc.gpsimd.dma_start(out=rows[s][0:15, :], in_=biases[s].rearrange("(c n) -> c n", n=BANK))
+            if s == A:
+                make_identity(nc, ident[:])
+            nc.gpsimd.dma_start(out=f_raw[s][:], in_=rope_rows[first_pos[s] : first_pos[s] + TOKENS, :])
+            for t in (Q, K):
+                nc.gpsimd.dma_start(out=gain_rows[s][t : t + 1, :], in_=gains[s][t].unsqueeze(0))
+        clear(nc.vector, planes[1])
+        clear(nc.vector, planes[2])
+        clear(nc.vector, xs[B])
+        clear(nc.gpsimd, planes[3])
+        for g in range(2, PASSES):
+            load_codes(0, g)
+        load_scales(1)
+        load_scales(2)
+        load_unit(1)
+        load_tokens(B)
+        load_token_scales(B)
+        load_unit(2)
+
+        loads_behind = {
+            0: lambda: (load_scales(3), load_scales(4), load_unit(3)),
+            1: lambda: (load_unit(4), load_scales(5)),
+            2: lambda: load_unit(5),
+        }
+        group = 0
+        for i in range(3):
+            spread(group)
+            group += 1
+        parts = []
+        for u in range(len(UNITS)):
+            banks = new_banks()
+            for g in range(PASSES):
+                if g == 0 and u < 2:
+                    for t in (Q, K):
+                        make_table(u, t)
+                if group < 15:
+                    spread(group)
+                    group += 1
+                multiply(u, banks, g)
+                if parts:
+                    parts[g]()
+            if u in loads_behind:
+                loads_behind[u]()
+            parts = epilogue_v(u, banks) if UNITS[u][1] == V else epilogue_qk(u, banks)
+        for part in parts:
+            part()

@@ -48,6 +48,7 @@ def tile_fluxjointattention_pa_kernel(
     with ExitStack() as ctx:
         keep = ctx.enter_context(tc.tile_pool(name="keep", bufs=1))
         work = ctx.enter_context(tc.tile_pool(name="work", bufs=2))
+        single = ctx.enter_context(tc.tile_pool(name="single", bufs=1))
         result = ctx.enter_context(tc.tile_pool(name="result", bufs=3))
         stats = ctx.enter_context(tc.tile_pool(name="stats", bufs=4))
         acc_pool = ctx.enter_context(tc.psum_pool(name="acc", bufs=6))
@@ -60,10 +61,10 @@ def tile_fluxjointattention_pa_kernel(
         planes = [keep.tile([P, PASSES * D], U8, name="plane%d" % i, align_bytes=256) for i in range(PLANES)]
         rows = [keep.tile([P, BANK], BF16, name="rows%d" % s) for s in (A, B)]
         gain_rows = [keep.tile([P, DH], BF16, name="gain_rows%d" % s) for s in (A, B)]
-        bias = keep.tile([P, 2 * 3 * D], BF16, name="bias")
+        bias = [keep.tile([P, D], BF16, name="bias%d" % u) for u in range(len(UNITS))]
         ident = keep.tile([P, P], BF16, name="ident")
         f_raw = [keep.tile([P, 4 * PAIRS], BF16, name="f_raw%d" % s) for s in (A, B)]
-        tables = [[keep.tile([P, 2, PAIRS, 2], F32, name="table%d%d" % (s, t)) for t in (Q, K)] for s in (A, B)]
+        tables = [[keep.tile([P, 2, 2, PAIRS], F32, name="table%d%d" % (s, t)) for t in (Q, K)] for s in (A, B)]
 
         def clear(engine, t):
             engine.memset(t[:].bitcast(I32), 0)
@@ -100,17 +101,31 @@ def tile_fluxjointattention_pa_kernel(
             for g in range(PASSES):
                 load_codes(u, g)
 
-        row_order = [(s, kind * BANKS + i) for s, kind in UNITS for i in range(BANKS)]
+        groups = [(u, b, min(2, BANKS - b)) for u in range(len(UNITS)) for b in range(0, BANKS, 2)]
 
-        def spread(group):
+        def split(ap):
+            return ap.rearrange("p (i n) -> p i n", i=2)
+
+        def pairs(ap):
+            return ap.rearrange("p (n i) -> p i n", i=2)
+
+        def columns(u, ap, b, count):
+            if UNITS[u][1] == V:
+                return ap[:, b * BANK : (b + count) * BANK]
+            return split(ap)[:, :, b * BANK // 2 : (b + count) * BANK // 2]
+
+        def spread():
+            u, b, count = groups.pop(0)
+            s, kind = UNITS[u]
             bank = row_pool.tile([P, GROUP], BF16, name="row")
-            for i in range(2):
-                s, c = row_order[2 * group + i]
+            for i in range(count):
+                c = kind * BANKS + b + i
                 nc.tensor.matmul(
                     bank[:, i * BANK : (i + 1) * BANK],
                     lhsT=ident[:, c : c + 1].to_broadcast([P, P]), rhs=rows[s][:], start=True, stop=True,
                 )
-            nc.scalar.copy(out=bias[:, group * GROUP : (group + 1) * GROUP], in_=bank[:])
+            got = bank[:, : count * BANK]
+            nc.scalar.copy(out=columns(u, bias[u][:], b, count), in_=got if kind == V else pairs(got))
 
         def make_table(s, t):
             bank = row_pool.tile([P, BANK], F32, name="row")
@@ -119,14 +134,14 @@ def tile_fluxjointattention_pa_kernel(
             )
             nc.vector.tensor_tensor(
                 out=tables[s][t][:],
-                in0=f_raw[s][:].rearrange("p (j i t) -> p t j i", i=2, t=2),
-                in1=bank[:, :DH].rearrange("p (j t) -> p t j", t=2).unsqueeze(3).to_broadcast([P, 2, PAIRS, 2]),
+                in0=f_raw[s][:].rearrange("p (j i t) -> p t i j", i=2, t=2),
+                in1=bank[:, :DH].rearrange("p (j t) -> p t j", t=2).unsqueeze(2).to_broadcast([P, 2, 2, PAIRS]),
                 op=ALU.mult,
             )
 
-        def multiply(u, banks, g):
+        def multiply(u, banks, which, passes):
             s, kind = UNITS[u]
-            for b in range(BANKS):
+            for b, g in ((b, g) for b in which for g in passes):
                 at = g * D + b * BANK
                 nc.tensor.matmul_mx(
                     out=banks[b][:],
@@ -154,12 +169,9 @@ def tile_fluxjointattention_pa_kernel(
 
         def add_bias(u, banks, y, b):
             nc.vector.tensor_tensor(
-                out=y[:, b * BANK : (b + 1) * BANK], in0=banks[b][:],
-                in1=bias[:, u * D + b * BANK : u * D + (b + 1) * BANK], op=ALU.add,
+                out=columns(u, y[:], b, 1), in0=banks[b][:] if UNITS[u][1] == V else pairs(banks[b][:]),
+                in1=columns(u, bias[u][:], b, 1), op=ALU.add,
             )
-
-        def head_view(ap):
-            return ap.rearrange("p (h j i) -> p h j i", j=PAIRS, i=2)
 
         def epilogue_v(u, banks):
             y = work.tile([P, D], F32, name="y")
@@ -180,15 +192,16 @@ def tile_fluxjointattention_pa_kernel(
             ss = stats.tile([P, HEADS], F32, name="ss")
             rs = stats.tile([P, HEADS], F32, name="rs")
             table = tables[s][kind]
-            shape = [P, HALF, PAIRS, 2]
+            shape = [P, 2, HALF, PAIRS]
             width = HALF * DH
             halves = []
 
             def squares(half):
                 for h in range(half * HALF, (half + 1) * HALF):
-                    junk = work.tile([P, DH], BF16, name="junk")
+                    junk = work.tile([P, 2, PAIRS], BF16, name="junk")
                     nc.scalar.activation(
-                        out=junk[:], in_=y[:, h * DH : (h + 1) * DH], func=ACT.Square, accum_out=ss[:, h : h + 1]
+                        out=junk[:], in_=split(y[:])[:, :, h * PAIRS : (h + 1) * PAIRS], func=ACT.Square,
+                        accum_out=ss[:, h : h + 1],
                     )
                 hs = slice(half * HALF, (half + 1) * HALF)
                 nc.scalar.activation(
@@ -196,31 +209,34 @@ def tile_fluxjointattention_pa_kernel(
                 )
 
             def product(half, t, dst):
+                at = t * D // 2 + half * HALF * PAIRS
                 nc.vector.tensor_tensor(
-                    out=head_view(dst[:]),
-                    in0=head_view(y[:, half * width : (half + 1) * width])[:, :, :, t : t + 1].to_broadcast(shape),
-                    in1=table[:, t, :, :].unsqueeze(1).to_broadcast(shape),
+                    out=dst[:].rearrange("p (i h j) -> p i h j", i=2, h=HALF),
+                    in0=y[:, at : at + HALF * PAIRS].rearrange("p (h j) -> p h j", h=HALF).unsqueeze(1).to_broadcast(shape),
+                    in1=table[:, t, :, :].unsqueeze(2).to_broadcast(shape),
                     op=ALU.mult,
                 )
 
             def finish(half):
-                res, odd = halves[half]
-                nc.vector.tensor_tensor(out=res[:], in0=res[:], in1=odd[:], op=ALU.add)
+                rot, odd = halves[half]
+                nc.vector.tensor_tensor(out=rot[:], in0=rot[:], in1=odd[:], op=ALU.add)
 
             def scale_and_store(half):
-                res, odd = halves[half]
+                rot, odd = halves[half]
+                res = result.tile([P, width], F32, name="res")
                 for i in range(HALF):
                     h = half * HALF + i
                     nc.scalar.activation(
-                        out=res[:, i * DH : (i + 1) * DH], in_=res[:, i * DH : (i + 1) * DH],
+                        out=res[:, i * DH : (i + 1) * DH].rearrange("p (j i) -> p j i", i=2),
+                        in_=split(rot[:])[:, :, i * PAIRS : (i + 1) * PAIRS].rearrange("p i j -> p j i"),
                         func=ACT.Copy, scale=rs[:, h : h + 1],
                     )
                 store(u, half * HALF, (half + 1) * HALF, res[:], nc.gpsimd)
 
             def start_half(half):
-                res = result.tile([P, width], F32, name="res")
-                odd = work.tile([P, width], F32, name="odd")
-                halves.append((res, odd))
+                rot = work.tile([P, width], F32, name="rot")
+                odd = single.tile([P, width], F32, name="odd")
+                halves.append((rot, odd))
 
             def part0():
                 for b in range(BANKS):
@@ -265,17 +281,17 @@ def tile_fluxjointattention_pa_kernel(
             nc.gpsimd.dma_start(out=f_raw[s][:], in_=rope_rows[first_pos[s] : first_pos[s] + TOKENS, :])
             for t in (Q, K):
                 nc.gpsimd.dma_start(out=gain_rows[s][t : t + 1, :], in_=gains[s][t].unsqueeze(0))
+        clear(nc.vector, xs[B])
         clear(nc.vector, planes[1])
         clear(nc.vector, planes[2])
-        clear(nc.vector, xs[B])
         clear(nc.gpsimd, planes[3])
         for g in range(2, PASSES):
             load_codes(0, g)
         load_scales(1)
         load_scales(2)
-        load_unit(1)
         load_tokens(B)
         load_token_scales(B)
+        load_unit(1)
         load_unit(2)
 
         loads_behind = {
@@ -283,23 +299,26 @@ def tile_fluxjointattention_pa_kernel(
             1: lambda: (load_unit(4), load_scales(5)),
             2: lambda: load_unit(5),
         }
-        group = 0
         for i in range(3):
-            spread(group)
-            group += 1
+            spread()
         parts = []
         for u in range(len(UNITS)):
             banks = new_banks()
             for g in range(PASSES):
-                if g == 0 and u < 2:
+                if u == 0 and g == 3:
                     for t in (Q, K):
-                        make_table(u, t)
-                if group < 15:
-                    spread(group)
-                    group += 1
-                multiply(u, banks, g)
+                        make_table(A, t)
+                if groups:
+                    spread()
+                if u in (0, len(UNITS) - 1):
+                    multiply(u, banks, range(BANKS), [g])
+                else:
+                    multiply(u, banks, [g], range(PASSES))
                 if parts:
                     parts[g]()
+            if u == 0:
+                for t in (Q, K):
+                    make_table(B, t)
             if u in loads_behind:
                 loads_behind[u]()
             parts = epilogue_v(u, banks) if UNITS[u][1] == V else epilogue_qk(u, banks)

from contextlib import ExitStack

import concourse.mybir as mybir
from concourse.masks import make_identity

F32 = mybir.dt.float32
BF16 = mybir.dt.bfloat16
I32 = mybir.dt.int32
U8 = mybir.dt.uint8
FP4X4 = mybir.dt.float4_e2m1fn_x4
ACT = mybir.ActivationFunctionType
ALU = mybir.AluOpType

P = 128
TOKENS = 128
D = 2560
HEADS = 8
DH = 320
PAIRS = DH // 2
HALF = HEADS // 2
EPS = 1e-6
PASSES = D // 512
BANK = 512
BANKS = D // BANK
GROUP = 2 * BANK

FLOPS = 2 * 2 * TOKENS * D * 3 * D

Q, K, V = 0, 1, 2
A, B = 0, 1
UNITS = [(A, Q), (A, K), (B, Q), (B, K), (A, V), (B, V)]
SLOTS = 3
PLANES = 4


def tile_fluxjointattention_pa_kernel(
    tc, xa_words, xa_scales, xb_words, xb_scales, rope, wa_words, wa_scales, a_bias,
    wb_words, wb_scales, b_bias, gain_qa, gain_ka, gain_qb, gain_kb, out_q, out_k, out_v,
):
    nc = tc.nc
    x_words, x_scales = (xa_words, xb_words), (xa_scales, xb_scales)
    w_words, w_scales = (wa_words, wb_words), (wa_scales, wb_scales)
    biases = (a_bias, b_bias)
    outs = (out_q, out_k, out_v)
    first_pos = (TOKENS, 0)
    gains = ((gain_qa, gain_ka), (gain_qb, gain_kb))

    with ExitStack() as ctx:
        keep = ctx.enter_context(tc.tile_pool(name="keep", bufs=1))
        work = ctx.enter_context(tc.tile_pool(name="work", bufs=2))
        single = ctx.enter_context(tc.tile_pool(name="single", bufs=1))
        result = ctx.enter_context(tc.tile_pool(name="result", bufs=3))
        stats = ctx.enter_context(tc.tile_pool(name="stats", bufs=4))
        acc_pool = ctx.enter_context(tc.psum_pool(name="acc", bufs=6))
        row_pool = ctx.enter_context(tc.psum_pool(name="rowbank", bufs=2))
        ctx.enter_context(tc.manual_schedule())

        xw = [keep.tile([P, PASSES * 2 * TOKENS], U8, name="xw%d" % s, align_bytes=256) for s in (A, B)]
        xs = [keep.tile([P, PASSES * TOKENS], U8, name="xs%d" % s, align_bytes=256) for s in (A, B)]
        codes = [keep.tile([P, PASSES * 2 * D], U8, name="codes%d" % i, align_bytes=256) for i in range(SLOTS)]
        planes = [keep.tile([P, PASSES * D], U8, name="plane%d" % i, align_bytes=256) for i in range(PLANES)]
        rows = [keep.tile([P, BANK], BF16, name="rows%d" % s) for s in (A, B)]
        gain_rows = [keep.tile([P, DH], BF16, name="gain_rows%d" % s) for s in (A, B)]
        bias = [keep.tile([P, D], BF16, name="bias%d" % u) for u in range(len(UNITS))]
        ident = keep.tile([P, P], BF16, name="ident")
        f_raw = [keep.tile([P, 4 * PAIRS], BF16, name="f_raw%d" % s) for s in (A, B)]
        tables = [[keep.tile([P, 2, 2, PAIRS], F32, name="table%d%d" % (s, t)) for t in (Q, K)] for s in (A, B)]

        def clear(engine, t):
            engine.memset(t[:].bitcast(I32), 0)

        def by_pass(ap):
            return ap.rearrange("p (g n) -> p g n", g=PASSES).bitcast(I32)

        def load_tokens(s):
            nc.sync.dma_start(out=by_pass(xw[s][:]), in_=x_words[s].rearrange("g p n -> p g n").bitcast(I32))

        def load_token_scales(s):
            for q in range(4):
                nc.sync.dma_start(
                    out=by_pass(xs[s][32 * q : 32 * q + 4, :]),
                    in_=x_scales[s][:, 4 * q : 4 * q + 4, :].rearrange("g q n -> q g n").bitcast(I32),
                )

        def load_codes(u, g):
            s, kind = UNITS[u]
            nc.sync.dma_start(
                out=codes[u % SLOTS][:, 2 * D * g : 2 * D * (g + 1)].bitcast(I32),
                in_=w_words[s][g, :, 2 * D * kind : 2 * D * (kind + 1)].bitcast(I32),
            )

        def load_scales(u, rs=range(4)):
            s, kind = UNITS[u]
            for r in rs:
                nc.sync.dma_start(
                    out=by_pass(planes[u % PLANES][r : P : 32, :]),
                    in_=w_scales[s][:, r : 16 : 4, D * kind : D * (kind + 1)].rearrange("g q n -> q g n").bitcast(I32),
                )

        def load_unit(u):
            for g in range(PASSES):
                load_codes(u, g)

        groups = [(u, b, min(2, BANKS - b)) for u in range(len(UNITS)) for b in range(0, BANKS, 2)]

        def split(ap):
            return ap.rearrange("p (i n) -> p i n", i=2)

        def pairs(ap):
            return ap.rearrange("p (n i) -> p i n", i=2)

        def columns(u, ap, b, count):
            if UNITS[u][1] == V:
                return ap[:, b * BANK : (b + count) * BANK]
            return split(ap)[:, :, b * BANK // 2 : (b + count) * BANK // 2]

        def spread():
            u, b, count = groups.pop(0)
            s, kind = UNITS[u]
            bank = row_pool.tile([P, GROUP], BF16, name="row")
            for i in range(count):
                c = kind * BANKS + b + i
                nc.tensor.matmul(
                    bank[:, i * BANK : (i + 1) * BANK],
                    lhsT=ident[:, c : c + 1].to_broadcast([P, P]), rhs=rows[s][:], start=True, stop=True,
                )
            got = bank[:, : count * BANK]
            nc.scalar.copy(out=columns(u, bias[u][:], b, count), in_=got if kind == V else pairs(got))

        def make_table(s, t):
            bank = row_pool.tile([P, BANK], F32, name="row")
            nc.tensor.matmul(
                bank[:, :DH], lhsT=ident[:, t : t + 1].to_broadcast([P, P]), rhs=gain_rows[s][:], start=True, stop=True
            )
            nc.vector.tensor_tensor(
                out=tables[s][t][:],
                in0=f_raw[s][:].rearrange("p (j i t) -> p t i j", i=2, t=2),
                in1=bank[:, :DH].rearrange("p (j t) -> p t j", t=2).unsqueeze(2).to_broadcast([P, 2, 2, PAIRS]),
                op=ALU.mult,
            )

        def multiply(u, banks, which, passes):
            s, kind = UNITS[u]
            for b, g in ((b, g) for b in which for g in passes):
                at = g * D + b * BANK
                nc.tensor.matmul_mx(
                    out=banks[b][:],
                    lhsT=xw[s][:, 2 * TOKENS * g : 2 * TOKENS * (g + 1)].bitcast(FP4X4),
                    lhsT_scale=xs[s][:, TOKENS * g : TOKENS * (g + 1)],
                    rhs=codes[u % SLOTS][:, 2 * at : 2 * (at + BANK)].bitcast(FP4X4),
                    rhs_scale=planes[u % PLANES][:, at : at + BANK],
                    start=(g == 0), stop=(g == PASSES - 1),
                )

        def new_banks():
            banks = []
            for b in range(BANKS):
                acc = acc_pool.tile([P, BANK], F32, name="acc")
                banks.append(acc)
            return banks

        def store(u, h0, h1, tile, engine):
            s, kind = UNITS[u]
            p0 = first_pos[s]
            engine.dma_start(
                out=outs[kind][0, h0:h1, p0 : p0 + TOKENS, :].rearrange("h p d -> p h d"),
                in_=tile.rearrange("p (h d) -> p h d", d=DH),
            )

        def add_bias(u, banks, y, b):
            nc.vector.tensor_tensor(
                out=columns(u, y[:], b, 1), in0=banks[b][:] if UNITS[u][1] == V else pairs(banks[b][:]),
                in1=columns(u, bias[u][:], b, 1), op=ALU.add,
            )

        def epilogue_v(u, banks):
            y = work.tile([P, D], F32, name="y")
            engine = nc.sync if u == len(UNITS) - 1 else nc.gpsimd
            stores = {1: (0, 3), 3: (3, 6), 4: (6, 8)}

            def part(b):
                add_bias(u, banks, y, b)
                if b in stores:
                    h0, h1 = stores[b]
                    store(u, h0, h1, y[:, h0 * DH : h1 * DH], engine)

            return [lambda b=b: part(b) for b in range(BANKS)]

        def epilogue_qk(u, banks):
            s, kind = UNITS[u]
            y = work.tile([P, D], F32, name="y")
            ss = stats.tile([P, HEADS], F32, name="ss")
            rs = stats.tile([P, HEADS], F32, name="rs")
            table = tables[s][kind]
            shape = [P, 2, HALF, PAIRS]
            width = HALF * DH
            halves = []

            def squares(half):
                for h in range(half * HALF, (half + 1) * HALF):
                    junk = work.tile([P, 2, PAIRS], BF16, name="junk")
                    nc.scalar.activation(
                        out=junk[:], in_=split(y[:])[:, :, h * PAIRS : (h + 1) * PAIRS], func=ACT.Square,
                        accum_out=ss[:, h : h + 1],
                    )
                hs = slice(half * HALF, (half + 1) * HALF)
                nc.scalar.activation(
                    out=rs[:, hs], in_=ss[:, hs], func=ACT.Abs_reciprocal_sqrt, scale=1.0 / DH, bias=EPS
                )

            def product(half, t, dst):
                at = t * D // 2 + half * HALF * PAIRS
                nc.vector.tensor_tensor(
                    out=dst[:].rearrange("p (i h j) -> p i h j", i=2, h=HALF),
                    in0=y[:, at : at + HALF * PAIRS].rearrange("p (h j) -> p h j", h=HALF).unsqueeze(1).to_broadcast(shape),
                    in1=table[:, t, :, :].unsqueeze(2).to_broadcast(shape),
                    op=ALU.mult,
                )

            def finish(half):
                rot, odd = halves[half]
                nc.vector.tensor_tensor(out=rot[:], in0=rot[:], in1=odd[:], op=ALU.add)

            def scale_and_store(half):
                rot, odd = halves[half]
                res = result.tile([P, width], F32, name="res")
                for i in range(HALF):
                    h = half * HALF + i
                    nc.scalar.activation(
                        out=res[:, i * DH : (i + 1) * DH].rearrange("p (j i) -> p j i", i=2),
                        in_=split(rot[:])[:, :, i * PAIRS : (i + 1) * PAIRS].rearrange("p i j -> p j i"),
                        func=ACT.Copy, scale=rs[:, h : h + 1],
                    )
                store(u, half * HALF, (half + 1) * HALF, res[:], nc.gpsimd)

            def start_half(half):
                rot = work.tile([P, width], F32, name="rot")
                odd = single.tile([P, width], F32, name="odd")
                halves.append((rot, odd))

            def part0():
                for b in range(BANKS):
                    add_bias(u, banks, y, b)
                squares(0)

            def part1():
                start_half(0)
                product(0, 0, halves[0][0])
                product(0, 1, halves[0][1])
                squares(1)

            def part2():
                start_half(1)
                product(1, 0, halves[1][0])
                finish(0)
                scale_and_store(0)

            def part3():
                product(1, 1, halves[1][1])
                finish(1)

            def part4():
                scale_and_store(1)

            return [part0, part1, part2, part3, part4]

        load_tokens(A)
        load_codes(0, 0)
        clear(nc.vector, xs[A])
        for t in rows + gain_rows:
            nc.vector.memset(t[:], 0.0)
        clear(nc.vector, planes[0])
        load_token_scales(A)
        load_codes(0, 1)
        load_scales(0)
        rope_rows = rope.rearrange("o u s j i t -> (o u s) (j i t)")
        for s in (A, B):
            nc.gpsimd.dma_start(out=rows[s][0:15, :], in_=biases[s].rearrange("(c n) -> c n", n=BANK))
            if s == A:
                make_identity(nc, ident[:])
            nc.gpsimd.dma_start(out=f_raw[s][:], in_=rope_rows[first_pos[s] : first_pos[s] + TOKENS, :])
            for t in (Q, K):
                nc.gpsimd.dma_start(out=gain_rows[s][t : t + 1, :], in_=gains[s][t].unsqueeze(0))
        clear(nc.vector, xs[B])
        clear(nc.vector, planes[1])
        clear(nc.vector, planes[2])
        clear(nc.gpsimd, planes[3])
        for g in range(2, PASSES):
            load_codes(0, g)
        load_scales(1)
        load_scales(2)
        load_tokens(B)
        load_token_scales(B)
        load_unit(1)
        load_unit(2)

        loads_behind = {
            0: lambda: (load_scales(3), load_scales(4), load_unit(3)),
            1: lambda: (load_unit(4), load_scales(5)),
            2: lambda: load_unit(5),
        }
        for i in range(3):
            spread()
        parts = []
        for u in range(len(UNITS)):
            banks = new_banks()
            for g in range(PASSES):
                if u == 0 and g == 3:
                    for t in (Q, K):
                        make_table(A, t)
                if groups:
                    spread()
                if u in (0, len(UNITS) - 1):
                    multiply(u, banks, range(BANKS), [g])
                else:
                    multiply(u, banks, [g], range(PASSES))
                if parts:
                    parts[g]()
            if u == 0:
                for t in (Q, K):
                    make_table(B, t)
            if u in loads_behind:
                loads_behind[u]()
            parts = epilogue_v(u, banks) if UNITS[u][1] == V else epilogue_qk(u, banks)
        for part in parts:
            part()
